import numpy as np
import ml_dtypes

BF16 = ml_dtypes.bfloat16


def bf(x):
    return np.asarray(x, np.float32).astype(BF16)


def f32(x):
    return np.asarray(x, np.float32)


def f64(x):
    return np.asarray(x).astype(np.float64)


def striped(idx):
    return np.tile(idx.reshape(-1, 16).T, (8, 1))


S, HD, M, N = 512, 128, 256, 128
EPS = 1e-6
SCALE = HD ** -0.5


def setup_inputs():
    return {"k_cache": bf(1.5 * np.random.standard_normal((S, HD))), "q": bf(np.random.standard_normal((HD, M)) * (0.5 + np.random.random((1, M)))), "v": bf(np.random.standard_normal((N, HD))), "offs": striped(np.random.permutation(S)[:N])}


def reference(k_cache, q, v, offs):
    idx = offs[:16].T.reshape(-1)
    qq = f64(q)
    r = 1.0 / np.sqrt(np.mean(qq * qq, axis=0) + EPS)
    s = SCALE * r[:, None] * (qq.T @ f64(k_cache)[idx].T)
    e = np.exp(s - s.max(axis=1, keepdims=True))
    p = e / e.sum(axis=1, keepdims=True)
    return p @ f64(v)

@@ -1,0 +1,78 @@
+import concourse.mybir as mybir
+from concourse.masks import make_identity
+
+BF16, F32, U16 = mybir.dt.bfloat16, mybir.dt.float32, mybir.dt.uint16
+MULT, ADD, POW = mybir.AluOpType.mult, mybir.AluOpType.add, mybir.AluOpType.pow
+EXP = mybir.ActivationFunctionType.Exp
+X = mybir.AxisListType.X
+
+P = 128
+S, HD, M, N = 512, 128, 256, 128
+EPS = 1e-6
+FLOPS = 2 * M * N * HD * 2
+
+
+def tile_selfattention_kernel(tc, k_cache, q, v, offs, out):
+    nc = tc.nc
+    with (
+        tc.tile_pool(name="held", bufs=1) as held,
+        tc.tile_pool(name="work", bufs=2) as work,
+        tc.psum_pool(name="once", bufs=1) as once,
+        tc.psum_pool(name="block", bufs=2) as block,
+    ):
+        offsets = held.tile([P, N // 16], U16, name="offsets")
+        nc.sync.dma_start(offsets[:], offs)
+        key_rows = held.tile([P, S // P, HD], BF16, name="key_rows")
+        nc.sync.dma_start(key_rows[:], k_cache.rearrange("(c p) d -> p c d", p=P))
+        queries = held.tile([HD, M], BF16, name="queries")
+        nc.scalar.dma_start(queries[:], q)
+        values = held.tile([N, HD], BF16, name="values")
+        nc.scalar.dma_start(values[:], v)
+
+        identity = held.tile([P, P], BF16, name="identity")
+        make_identity(nc, identity[:])
+        ones = held.tile([HD, 1], F32, name="ones")
+        nc.vector.memset(ones[:], 1.0)
+        minus_half = held.tile([P, M // P], F32, name="minus_half")
+        nc.vector.memset(minus_half[:], -0.5)
+
+        flipped_keys = once.tile([HD, S], BF16, name="flipped_keys")
+        for c in range(S // P):
+            nc.tensor.transpose(flipped_keys[:, c * P : (c + 1) * P], key_rows[:, c, :], identity[:])
+        key_window = held.tile([HD, S], BF16, name="key_window")
+        nc.vector.tensor_copy(key_window[:], flipped_keys[:])
+
+        squares = held.tile([HD, M], F32, name="squares")
+        nc.vector.tensor_tensor(squares[:], queries[:], queries[:], MULT)
+        square_sums = once.tile([P, M // P], F32, name="square_sums")
+        for b in range(M // P):
+            nc.tensor.matmul(square_sums[:, b : b + 1], squares[:, b * P : (b + 1) * P], ones[:], start=True, stop=True)
+        shifted_sums = held.tile([P, M // P], F32, name="shifted_sums")
+        nc.vector.tensor_scalar_add(shifted_sums[:], square_sums[:], HD * EPS)
+        query_scale = held.tile([P, M // P], F32, name="query_scale")
+        nc.gpsimd.tensor_tensor(query_scale[:], shifted_sums[:], minus_half[:], POW)
+
+        for b in range(M // P):
+            scale_b = query_scale[:, b : b + 1]
+            raw = block.tile([P, N], F32, name="raw")
+            nc.tensor.matmul(
+                raw[:], queries[:, b * P : (b + 1) * P], key_window[:].indirect(offsets[:]), start=True, stop=True
+            )
+            raw_max = work.tile([P, 1], F32, name="raw_max")
+            nc.vector.reduce_max(raw_max[:], raw[:], axis=X)
+            minus_max = work.tile([P, 1], F32, name="minus_max")
+            nc.vector.tensor_scalar(minus_max[:], raw_max[:], scale_b, -1.0, MULT, MULT)
+            weights = work.tile([P, N], BF16, name="weights")
+            weight_sum = work.tile([P, 1], F32, name="weight_sum")
+            nc.scalar.activation(weights[:], raw[:], EXP, bias=minus_max[:], scale=scale_b, accum_out=weight_sum[:])
+            inverse_sum = work.tile([P, 1], F32, name="inverse_sum")
+            nc.vector.reciprocal(inverse_sum[:], weight_sum[:])
+            flipped_weights = block.tile([N, P], BF16, name="flipped_weights")
+            nc.tensor.transpose(flipped_weights[:], weights[:], identity[:])
+            weights_by_entry = work.tile([N, P], BF16, name="weights_by_entry")
+            nc.vector.tensor_copy(weights_by_entry[:], flipped_weights[:])
+            mixed = block.tile([P, HD], F32, name="mixed")
+            nc.tensor.matmul(mixed[:], weights_by_entry[:], values[:], start=True, stop=True)
+            result = work.tile([P, HD], F32, name="result")
+            nc.vector.tensor_scalar_mul(result[:], mixed[:], inverse_sum[:])
+            nc.sync.dma_start(out[b * P : (b + 1) * P, :], result[:])

@@ -2,12 +2,14 @@ import concourse.mybir as mybir
 from concourse.masks import make_identity
 
 BF16, F32, U16 = mybir.dt.bfloat16, mybir.dt.float32, mybir.dt.uint16
-MULT, ADD, POW = mybir.AluOpType.mult, mybir.AluOpType.add, mybir.AluOpType.pow
-EXP = mybir.ActivationFunctionType.Exp
+MULT, POW = mybir.AluOpType.mult, mybir.AluOpType.pow
+EXP, SQUARE = mybir.ActivationFunctionType.Exp, mybir.ActivationFunctionType.Square
 X = mybir.AxisListType.X
 
 P = 128
 S, HD, M, N = 512, 128, 256, 128
+BLOCKS = M // P
+CHUNKS = S // P
 EPS = 1e-6
 FLOPS = 2 * M * N * HD * 2
 
@@ -16,63 +18,72 @@ def tile_selfattention_kernel(tc, k_cache, q, v, offs, out):
     nc = tc.nc
     with (
         tc.tile_pool(name="held", bufs=1) as held,
-        tc.tile_pool(name="work", bufs=2) as work,
-        tc.psum_pool(name="once", bufs=1) as once,
-        tc.psum_pool(name="block", bufs=2) as block,
+        tc.psum_pool(name="flip", bufs=2) as flip,
+        tc.psum_pool(name="acc", bufs=1) as acc,
     ):
-        offsets = held.tile([P, N // 16], U16, name="offsets")
-        nc.sync.dma_start(offsets[:], offs)
-        key_rows = held.tile([P, S // P, HD], BF16, name="key_rows")
-        nc.sync.dma_start(key_rows[:], k_cache.rearrange("(c p) d -> p c d", p=P))
         queries = held.tile([HD, M], BF16, name="queries")
         nc.scalar.dma_start(queries[:], q)
+        load_queue = (nc.sync, nc.scalar)
+        key_rows = [held.tile([P, HD], BF16, name=f"key_rows{c}") for c in range(CHUNKS)]
+        for c in range(CHUNKS):
+            load_queue[c % 2].dma_start(key_rows[c][:], k_cache[c * P : (c + 1) * P, :])
+        offsets = held.tile([P, N // 16], U16, name="offsets")
+        nc.sync.dma_start(offsets[:], offs)
         values = held.tile([N, HD], BF16, name="values")
-        nc.scalar.dma_start(values[:], v)
+        nc.sync.dma_start(values[:], v)
 
         identity = held.tile([P, P], BF16, name="identity")
         make_identity(nc, identity[:])
-        ones = held.tile([HD, 1], F32, name="ones")
-        nc.vector.memset(ones[:], 1.0)
-        minus_half = held.tile([P, M // P], F32, name="minus_half")
+        minus_half = held.tile([P, BLOCKS], F32, name="minus_half")
         nc.vector.memset(minus_half[:], -0.5)
 
-        flipped_keys = once.tile([HD, S], BF16, name="flipped_keys")
-        for c in range(S // P):
-            nc.tensor.transpose(flipped_keys[:, c * P : (c + 1) * P], key_rows[:, c, :], identity[:])
-        key_window = held.tile([HD, S], BF16, name="key_window")
-        nc.vector.tensor_copy(key_window[:], flipped_keys[:])
-
-        squares = held.tile([HD, M], F32, name="squares")
-        nc.vector.tensor_tensor(squares[:], queries[:], queries[:], MULT)
-        square_sums = once.tile([P, M // P], F32, name="square_sums")
-        for b in range(M // P):
-            nc.tensor.matmul(square_sums[:, b : b + 1], squares[:, b * P : (b + 1) * P], ones[:], start=True, stop=True)
-        shifted_sums = held.tile([P, M // P], F32, name="shifted_sums")
-        nc.vector.tensor_scalar_add(shifted_sums[:], square_sums[:], HD * EPS)
-        query_scale = held.tile([P, M // P], F32, name="query_scale")
+        square_sums = held.tile([P, BLOCKS], F32, name="square_sums")
+        for b in range(BLOCKS):
+            flipped_queries = flip.tile([P, HD], BF16, name=f"flipped_queries{b}", tag="flipped")
+            nc.tensor.transpose(flipped_queries[:], queries[:, b * P : (b + 1) * P], identity[:])
+            squares = held.tile([P, HD], BF16, name=f"squares{b}")
+            nc.scalar.activation(squares[:], flipped_queries[:], SQUARE, accum_out=square_sums[:, b : b + 1])
+        shifted_sums = held.tile([P, BLOCKS], F32, name="shifted_sums")
+        nc.scalar.add(shifted_sums[:], square_sums[:], HD * EPS)
+        query_scale = held.tile([P, BLOCKS], F32, name="query_scale")
         nc.gpsimd.tensor_tensor(query_scale[:], shifted_sums[:], minus_half[:], POW)
 
-        for b in range(M // P):
-            scale_b = query_scale[:, b : b + 1]
-            raw = block.tile([P, N], F32, name="raw")
+        key_window = held.tile([HD, S], BF16, name="key_window")
+        for h in range(CHUNKS // 2):
+            flipped_keys = acc.tile([HD, 2 * P], BF16, name=f"flipped_keys{h}")
+            for c in range(2):
+                nc.tensor.transpose(flipped_keys[:, c * P : (c + 1) * P], key_rows[2 * h + c][:], identity[:])
+            nc.vector.tensor_copy(key_window[:, h * 2 * P : (h + 1) * 2 * P], flipped_keys[:])
+
+        raw = [acc.tile([P, N], F32, name=f"raw{b}") for b in range(BLOCKS)]
+        for b in range(BLOCKS):
             nc.tensor.matmul(
-                raw[:], queries[:, b * P : (b + 1) * P], key_window[:].indirect(offsets[:]), start=True, stop=True
+                raw[b][:], queries[:, b * P : (b + 1) * P], key_window[:].indirect(offsets[:]), start=True, stop=True
             )
-            raw_max = work.tile([P, 1], F32, name="raw_max")
-            nc.vector.reduce_max(raw_max[:], raw[:], axis=X)
-            minus_max = work.tile([P, 1], F32, name="minus_max")
-            nc.vector.tensor_scalar(minus_max[:], raw_max[:], scale_b, -1.0, MULT, MULT)
-            weights = work.tile([P, N], BF16, name="weights")
-            weight_sum = work.tile([P, 1], F32, name="weight_sum")
-            nc.scalar.activation(weights[:], raw[:], EXP, bias=minus_max[:], scale=scale_b, accum_out=weight_sum[:])
-            inverse_sum = work.tile([P, 1], F32, name="inverse_sum")
-            nc.vector.reciprocal(inverse_sum[:], weight_sum[:])
-            flipped_weights = block.tile([N, P], BF16, name="flipped_weights")
-            nc.tensor.transpose(flipped_weights[:], weights[:], identity[:])
-            weights_by_entry = work.tile([N, P], BF16, name="weights_by_entry")
-            nc.vector.tensor_copy(weights_by_entry[:], flipped_weights[:])
-            mixed = block.tile([P, HD], F32, name="mixed")
-            nc.tensor.matmul(mixed[:], weights_by_entry[:], values[:], start=True, stop=True)
-            result = work.tile([P, HD], F32, name="result")
-            nc.vector.tensor_scalar_mul(result[:], mixed[:], inverse_sum[:])
-            nc.sync.dma_start(out[b * P : (b + 1) * P, :], result[:])
+        minus_max = [held.tile([P, 1], F32, name=f"minus_max{b}") for b in range(BLOCKS)]
+        for b in range(BLOCKS):
+            raw_max = held.tile([P, 1], F32, name=f"raw_max{b}")
+            nc.vector.reduce_max(raw_max[:], raw[b][:], axis=X)
+            nc.vector.tensor_scalar(minus_max[b][:], raw_max[:], query_scale[:, b : b + 1], -1.0, MULT, MULT)
+        weights = [held.tile([P, N], BF16, name=f"weights{b}") for b in range(BLOCKS)]
+        inverse_sum = [held.tile([P, 1], F32, name=f"inverse_sum{b}") for b in range(BLOCKS)]
+        for b in range(BLOCKS):
+            weight_sum = held.tile([P, 1], F32, name=f"weight_sum{b}")
+            nc.scalar.activation(
+                weights[b][:], raw[b][:], EXP,
+                bias=minus_max[b][:], scale=query_scale[:, b : b + 1], accum_out=weight_sum[:],
+            )
+            nc.vector.reciprocal(inverse_sum[b][:], weight_sum[:])
+        weights_by_entry = [held.tile([N, P], BF16, name=f"weights_by_entry{b}") for b in range(BLOCKS)]
+        for b in range(BLOCKS):
+            flipped_weights = flip.tile([N, P], BF16, name=f"flipped_weights{b}", tag="flipped")
+            nc.tensor.transpose(flipped_weights[:], weights[b][:], identity[:])
+            nc.vector.tensor_copy(weights_by_entry[b][:], flipped_weights[:])
+        mixed = [acc.tile([P, HD], F32, name=f"mixed{b}") for b in range(BLOCKS)]
+        for b in range(BLOCKS):
+            nc.tensor.matmul(mixed[b][:], weights_by_entry[b][:], values[:], start=True, stop=True)
+        store_queue = (nc.sync, nc.scalar)
+        for b in range(BLOCKS):
+            result = held.tile([P, HD], F32, name=f"result{b}")
+            nc.vector.tensor_scalar_mul(result[:], mixed[b][:], inverse_sum[b][:])
+            store_queue[b].dma_start(out[b * P : (b + 1) * P, :], result[:])

@@ -10,6 +10,8 @@ P = 128
 S, HD, M, N = 512, 128, 256, 128
 BLOCKS = M // P
 CHUNKS = S // P
+BANK = 512
+WARM_UP = 3
 EPS = 1e-6
 FLOPS = 2 * M * N * HD * 2
 
@@ -31,6 +33,12 @@ def tile_selfattention_kernel(tc, k_cache, q, v, offs, out):
         nc.sync.dma_start(offsets[:], offs)
         values = held.tile([N, HD], BF16, name="values")
         nc.sync.dma_start(values[:], v)
+
+        idle_work = held.tile([P, BANK], BF16, name="idle_work")
+        nc.gpsimd.memset(idle_work[:], 0.0)
+        idle_product = acc.tile([P, BANK], F32, name="idle_product", tag="mixed1")
+        for i in range(WARM_UP):
+            nc.tensor.matmul(idle_product[:], idle_work[:, :P], idle_work[:], start=True, stop=True)
 
         identity = held.tile([P, P], BF16, name="identity")
         make_identity(nc, identity[:])

@@ -2,16 +2,15 @@ import concourse.mybir as mybir
 from concourse.masks import make_identity
 
 BF16, F32, U16 = mybir.dt.bfloat16, mybir.dt.float32, mybir.dt.uint16
-MULT, POW = mybir.AluOpType.mult, mybir.AluOpType.pow
+MULT = mybir.AluOpType.mult
 EXP, SQUARE = mybir.ActivationFunctionType.Exp, mybir.ActivationFunctionType.Square
+RSQRT = mybir.ActivationFunctionType.Abs_reciprocal_sqrt
 X = mybir.AxisListType.X
 
 P = 128
 S, HD, M, N = 512, 128, 256, 128
 BLOCKS = M // P
 CHUNKS = S // P
-BANK = 512
-WARM_UP = 3
 EPS = 1e-6
 FLOPS = 2 * M * N * HD * 2
 
@@ -34,16 +33,13 @@ def tile_selfattention_kernel(tc, k_cache, q, v, offs, out):
         values = held.tile([N, HD], BF16, name="values")
         nc.sync.dma_start(values[:], v)
 
-        idle_work = held.tile([P, BANK], BF16, name="idle_work")
-        nc.gpsimd.memset(idle_work[:], 0.0)
-        idle_product = acc.tile([P, BANK], F32, name="idle_product", tag="mixed1")
-        for i in range(WARM_UP):
-            nc.tensor.matmul(idle_product[:], idle_work[:, :P], idle_work[:], start=True, stop=True)
-
         identity = held.tile([P, P], BF16, name="identity")
         make_identity(nc, identity[:])
-        minus_half = held.tile([P, BLOCKS], F32, name="minus_half")
-        nc.vector.memset(minus_half[:], -0.5)
+
+        one = held.tile([P, 1], F32, name="one")
+        nc.vector.memset(one[:], 1.0)
+        table_primer = held.tile([P, 1], F32, name="table_primer")
+        nc.scalar.activation(table_primer[:], one[:], RSQRT)
 
         square_sums = held.tile([P, BLOCKS], F32, name="square_sums")
         for b in range(BLOCKS):
@@ -51,10 +47,8 @@ def tile_selfattention_kernel(tc, k_cache, q, v, offs, out):
             nc.tensor.transpose(flipped_queries[:], queries[:, b * P : (b + 1) * P], identity[:])
             squares = held.tile([P, HD], BF16, name=f"squares{b}")
             nc.scalar.activation(squares[:], flipped_queries[:], SQUARE, accum_out=square_sums[:, b : b + 1])
-        shifted_sums = held.tile([P, BLOCKS], F32, name="shifted_sums")
-        nc.scalar.add(shifted_sums[:], square_sums[:], HD * EPS)
         query_scale = held.tile([P, BLOCKS], F32, name="query_scale")
-        nc.gpsimd.tensor_tensor(query_scale[:], shifted_sums[:], minus_half[:], POW)
+        nc.scalar.activation(query_scale[:], square_sums[:], RSQRT, bias=HD * EPS)
 
         key_window = held.tile([HD, S], BF16, name="key_window")
         for h in range(CHUNKS // 2):

@@ -2,10 +2,8 @@ import concourse.mybir as mybir
 from concourse.masks import make_identity
 
 BF16, F32, U16 = mybir.dt.bfloat16, mybir.dt.float32, mybir.dt.uint16
-MULT = mybir.AluOpType.mult
+MULT, MIN, POW = mybir.AluOpType.mult, mybir.AluOpType.min, mybir.AluOpType.pow
 EXP, SQUARE = mybir.ActivationFunctionType.Exp, mybir.ActivationFunctionType.Square
-RSQRT = mybir.ActivationFunctionType.Abs_reciprocal_sqrt
-X = mybir.AxisListType.X
 
 P = 128
 S, HD, M, N = 512, 128, 256, 128
@@ -35,11 +33,8 @@ def tile_selfattention_kernel(tc, k_cache, q, v, offs, out):
 
         identity = held.tile([P, P], BF16, name="identity")
         make_identity(nc, identity[:])
-
-        one = held.tile([P, 1], F32, name="one")
-        nc.vector.memset(one[:], 1.0)
-        table_primer = held.tile([P, 1], F32, name="table_primer")
-        nc.scalar.activation(table_primer[:], one[:], RSQRT)
+        minus_half = held.tile([P, BLOCKS], F32, name="minus_half")
+        nc.vector.memset(minus_half[:], -0.5)
 
         square_sums = held.tile([P, BLOCKS], F32, name="square_sums")
         for b in range(BLOCKS):
@@ -47,8 +42,12 @@ def tile_selfattention_kernel(tc, k_cache, q, v, offs, out):
             nc.tensor.transpose(flipped_queries[:], queries[:, b * P : (b + 1) * P], identity[:])
             squares = held.tile([P, HD], BF16, name=f"squares{b}")
             nc.scalar.activation(squares[:], flipped_queries[:], SQUARE, accum_out=square_sums[:, b : b + 1])
+        shifted_sums = held.tile([P, BLOCKS], F32, name="shifted_sums")
+        nc.scalar.add(shifted_sums[:], square_sums[:], HD * EPS)
         query_scale = held.tile([P, BLOCKS], F32, name="query_scale")
-        nc.scalar.activation(query_scale[:], square_sums[:], RSQRT, bias=HD * EPS)
+        nc.gpsimd.tensor_tensor(query_scale[:], shifted_sums[:], minus_half[:], POW)
+        minus_scale = held.tile([P, BLOCKS], F32, name="minus_scale")
+        nc.vector.tensor_scalar_mul(minus_scale[:], query_scale[:], -1.0)
 
         key_window = held.tile([HD, S], BF16, name="key_window")
         for h in range(CHUNKS // 2):
@@ -62,18 +61,18 @@ def tile_selfattention_kernel(tc, k_cache, q, v, offs, out):
             nc.tensor.matmul(
                 raw[b][:], queries[:, b * P : (b + 1) * P], key_window[:].indirect(offsets[:]), start=True, stop=True
             )
+        minus_scores = [held.tile([P, N], F32, name=f"minus_scores{b}") for b in range(BLOCKS)]
         minus_max = [held.tile([P, 1], F32, name=f"minus_max{b}") for b in range(BLOCKS)]
         for b in range(BLOCKS):
-            raw_max = held.tile([P, 1], F32, name=f"raw_max{b}")
-            nc.vector.reduce_max(raw_max[:], raw[b][:], axis=X)
-            nc.vector.tensor_scalar(minus_max[b][:], raw_max[:], query_scale[:, b : b + 1], -1.0, MULT, MULT)
+            nc.vector.tensor_scalar(
+                minus_scores[b][:], raw[b][:], minus_scale[:, b : b + 1], None, MULT, MIN, accum_out=minus_max[b][:]
+            )
         weights = [held.tile([P, N], BF16, name=f"weights{b}") for b in range(BLOCKS)]
         inverse_sum = [held.tile([P, 1], F32, name=f"inverse_sum{b}") for b in range(BLOCKS)]
         for b in range(BLOCKS):
             weight_sum = held.tile([P, 1], F32, name=f"weight_sum{b}")
             nc.scalar.activation(
-                weights[b][:], raw[b][:], EXP,
-                bias=minus_max[b][:], scale=query_scale[:, b : b + 1], accum_out=weight_sum[:],
+                weights[b][:], minus_scores[b][:], EXP, bias=minus_max[b][:], scale=-1.0, accum_out=weight_sum[:]
             )
             nc.vector.reciprocal(inverse_sum[b][:], weight_sum[:])
         weights_by_entry = [held.tile([N, P], BF16, name=f"weights_by_entry{b}") for b in range(BLOCKS)]

@@ -2,8 +2,14 @@ import concourse.mybir as mybir
 from concourse.masks import make_identity
 
 BF16, F32, U16 = mybir.dt.bfloat16, mybir.dt.float32, mybir.dt.uint16
-MULT, MIN, POW = mybir.AluOpType.mult, mybir.AluOpType.min, mybir.AluOpType.pow
-EXP, SQUARE = mybir.ActivationFunctionType.Exp, mybir.ActivationFunctionType.Square
+ADD, SUBTRACT, MULT, POW = (
+    mybir.AluOpType.add,
+    mybir.AluOpType.subtract,
+    mybir.AluOpType.mult,
+    mybir.AluOpType.pow,
+)
+EXP = mybir.ActivationFunctionType.Exp
+X = mybir.AxisListType.X
 
 P = 128
 S, HD, M, N = 512, 128, 256, 128
@@ -17,12 +23,12 @@ def tile_selfattention_kernel(tc, k_cache, q, v, offs, out):
     nc = tc.nc
     with (
         tc.tile_pool(name="held", bufs=1) as held,
-        tc.psum_pool(name="flip", bufs=2) as flip,
+        tc.psum_pool(name="turn", bufs=2) as turn,
         tc.psum_pool(name="acc", bufs=1) as acc,
     ):
         queries = held.tile([HD, M], BF16, name="queries")
-        nc.scalar.dma_start(queries[:], q)
-        load_queue = (nc.sync, nc.scalar)
+        nc.sync.dma_start(queries[:], q)
+        load_queue = (nc.scalar, nc.sync)
         key_rows = [held.tile([P, HD], BF16, name=f"key_rows{c}") for c in range(CHUNKS)]
         for c in range(CHUNKS):
             load_queue[c % 2].dma_start(key_rows[c][:], k_cache[c * P : (c + 1) * P, :])
@@ -36,18 +42,20 @@ def tile_selfattention_kernel(tc, k_cache, q, v, offs, out):
         minus_half = held.tile([P, BLOCKS], F32, name="minus_half")
         nc.vector.memset(minus_half[:], -0.5)
 
-        square_sums = held.tile([P, BLOCKS], F32, name="square_sums")
-        for b in range(BLOCKS):
-            flipped_queries = flip.tile([P, HD], BF16, name=f"flipped_queries{b}", tag="flipped")
-            nc.tensor.transpose(flipped_queries[:], queries[:, b * P : (b + 1) * P], identity[:])
-            squares = held.tile([P, HD], BF16, name=f"squares{b}")
-            nc.scalar.activation(squares[:], flipped_queries[:], SQUARE, accum_out=square_sums[:, b : b + 1])
+        table_primer = held.tile([P, BLOCKS], F32, name="table_primer")
+        nc.scalar.activation(table_primer[:], minus_half[:], EXP)
+
         shifted_sums = held.tile([P, BLOCKS], F32, name="shifted_sums")
-        nc.scalar.add(shifted_sums[:], square_sums[:], HD * EPS)
+        for b in range(BLOCKS):
+            q_b = queries[:, b * P : (b + 1) * P]
+            products = turn.tile([P, P], F32, name=f"products{b}", tag="turn")
+            nc.tensor.matmul(products[:], q_b, q_b, start=True, stop=True)
+            diagonal = held.tile([P, P], F32, name=f"diagonal{b}")
+            nc.vector.scalar_tensor_tensor(
+                diagonal[:], products[:], HD * EPS, identity[:], ADD, MULT, accum_out=shifted_sums[:, b : b + 1]
+            )
         query_scale = held.tile([P, BLOCKS], F32, name="query_scale")
         nc.gpsimd.tensor_tensor(query_scale[:], shifted_sums[:], minus_half[:], POW)
-        minus_scale = held.tile([P, BLOCKS], F32, name="minus_scale")
-        nc.vector.tensor_scalar_mul(minus_scale[:], query_scale[:], -1.0)
 
         key_window = held.tile([HD, S], BF16, name="key_window")
         for h in range(CHUNKS // 2):
@@ -61,23 +69,22 @@ def tile_selfattention_kernel(tc, k_cache, q, v, offs, out):
             nc.tensor.matmul(
                 raw[b][:], queries[:, b * P : (b + 1) * P], key_window[:].indirect(offsets[:]), start=True, stop=True
             )
-        minus_scores = [held.tile([P, N], F32, name=f"minus_scores{b}") for b in range(BLOCKS)]
-        minus_max = [held.tile([P, 1], F32, name=f"minus_max{b}") for b in range(BLOCKS)]
+        shifted = [held.tile([P, N], F32, name=f"shifted{b}") for b in range(BLOCKS)]
         for b in range(BLOCKS):
-            nc.vector.tensor_scalar(
-                minus_scores[b][:], raw[b][:], minus_scale[:, b : b + 1], None, MULT, MIN, accum_out=minus_max[b][:]
-            )
+            raw_max = held.tile([P, 1], F32, name=f"raw_max{b}")
+            nc.vector.reduce_max(raw_max[:], raw[b][:], axis=X)
+            nc.vector.tensor_scalar(shifted[b][:], raw[b][:], raw_max[:], None, SUBTRACT)
         weights = [held.tile([P, N], BF16, name=f"weights{b}") for b in range(BLOCKS)]
         inverse_sum = [held.tile([P, 1], F32, name=f"inverse_sum{b}") for b in range(BLOCKS)]
         for b in range(BLOCKS):
             weight_sum = held.tile([P, 1], F32, name=f"weight_sum{b}")
             nc.scalar.activation(
-                weights[b][:], minus_scores[b][:], EXP, bias=minus_max[b][:], scale=-1.0, accum_out=weight_sum[:]
+                weights[b][:], shifted[b][:], EXP, scale=query_scale[:, b : b + 1], accum_out=weight_sum[:]
             )
             nc.vector.reciprocal(inverse_sum[b][:], weight_sum[:])
         weights_by_entry = [held.tile([N, P], BF16, name=f"weights_by_entry{b}") for b in range(BLOCKS)]
         for b in range(BLOCKS):
-            flipped_weights = flip.tile([N, P], BF16, name=f"flipped_weights{b}", tag="flipped")
+            flipped_weights = turn.tile([N, P], BF16, name=f"flipped_weights{b}", tag="turn")
             nc.tensor.transpose(flipped_weights[:], weights[b][:], identity[:])
             nc.vector.tensor_copy(weights_by_entry[b][:], flipped_weights[:])
         mixed = [acc.tile([P, HD], F32, name=f"mixed{b}") for b in range(BLOCKS)]

@@ -2,9 +2,8 @@ import concourse.mybir as mybir
 from concourse.masks import make_identity
 
 BF16, F32, U16 = mybir.dt.bfloat16, mybir.dt.float32, mybir.dt.uint16
-ADD, SUBTRACT, MULT, POW = (
+ADD, MULT, POW = (
     mybir.AluOpType.add,
-    mybir.AluOpType.subtract,
     mybir.AluOpType.mult,
     mybir.AluOpType.pow,
 )
@@ -69,17 +68,22 @@ def tile_selfattention_kernel(tc, k_cache, q, v, offs, out):
             nc.tensor.matmul(
                 raw[b][:], queries[:, b * P : (b + 1) * P], key_window[:].indirect(offsets[:]), start=True, stop=True
             )
-        shifted = [held.tile([P, N], F32, name=f"shifted{b}") for b in range(BLOCKS)]
+        minus_max = [held.tile([P, 1], F32, name=f"minus_max{b}") for b in range(BLOCKS)]
         for b in range(BLOCKS):
             raw_max = held.tile([P, 1], F32, name=f"raw_max{b}")
             nc.vector.reduce_max(raw_max[:], raw[b][:], axis=X)
-            nc.vector.tensor_scalar(shifted[b][:], raw[b][:], raw_max[:], None, SUBTRACT)
+            nc.vector.tensor_scalar(minus_max[b][:], raw_max[:], query_scale[:, b : b + 1], -1.0, MULT, MULT)
         weights = [held.tile([P, N], BF16, name=f"weights{b}") for b in range(BLOCKS)]
         inverse_sum = [held.tile([P, 1], F32, name=f"inverse_sum{b}") for b in range(BLOCKS)]
         for b in range(BLOCKS):
             weight_sum = held.tile([P, 1], F32, name=f"weight_sum{b}")
             nc.scalar.activation(
-                weights[b][:], shifted[b][:], EXP, scale=query_scale[:, b : b + 1], accum_out=weight_sum[:]
+                weights[b][:],
+                raw[b][:],
+                EXP,
+                bias=minus_max[b][:],
+                scale=query_scale[:, b : b + 1],
+                accum_out=weight_sum[:],
             )
             nc.vector.reciprocal(inverse_sum[b][:], weight_sum[:])
         weights_by_entry = [held.tile([N, P], BF16, name=f"weights_by_entry{b}") for b in range(BLOCKS)]

@@ -94,8 +94,7 @@ def tile_selfattention_kernel(tc, k_cache, q, v, offs, out):
         mixed = [acc.tile([P, HD], F32, name=f"mixed{b}") for b in range(BLOCKS)]
         for b in range(BLOCKS):
             nc.tensor.matmul(mixed[b][:], weights_by_entry[b][:], values[:], start=True, stop=True)
-        store_queue = (nc.sync, nc.scalar)
         for b in range(BLOCKS):
             result = held.tile([P, HD], F32, name=f"result{b}")
             nc.vector.tensor_scalar_mul(result[:], mixed[b][:], inverse_sum[b][:])
-            store_queue[b].dma_start(out[b * P : (b + 1) * P, :], result[:])
+            nc.scalar.dma_start(out[b * P : (b + 1) * P, :], result[:])

@@ -94,7 +94,7 @@ def tile_selfattention_kernel(tc, k_cache, q, v, offs, out):
         mixed = [acc.tile([P, HD], F32, name=f"mixed{b}") for b in range(BLOCKS)]
         for b in range(BLOCKS):
             nc.tensor.matmul(mixed[b][:], weights_by_entry[b][:], values[:], start=True, stop=True)
+        result = held.tile([P, BLOCKS, HD], F32, name="result")
         for b in range(BLOCKS):
-            result = held.tile([P, HD], F32, name=f"result{b}")
-            nc.vector.tensor_scalar_mul(result[:], mixed[b][:], inverse_sum[b][:])
-            nc.scalar.dma_start(out[b * P : (b + 1) * P, :], result[:])
+            nc.vector.tensor_scalar_mul(result[:, b, :], mixed[b][:], inverse_sum[b][:])
+        nc.scalar.dma_start(out.rearrange("(b p) e -> p b e", p=P), result[:])

@@ -89,7 +89,7 @@ def tile_selfattention_kernel(tc, k_cache, q, v, offs, out):
         weights_by_entry = [held.tile([N, P], BF16, name=f"weights_by_entry{b}") for b in range(BLOCKS)]
         for b in range(BLOCKS):
             flipped_weights = turn.tile([N, P], BF16, name=f"flipped_weights{b}", tag="turn")
-            nc.tensor.transpose(flipped_weights[:], weights[b][:], identity[:])
+            nc.tensor.matmul(flipped_weights[:], weights[b][:], identity[:], start=True, stop=True)
             nc.vector.tensor_copy(weights_by_entry[b][:], flipped_weights[:])
         mixed = [acc.tile([P, HD], F32, name=f"mixed{b}") for b in range(BLOCKS)]
         for b in range(BLOCKS):

@@ -77,14 +77,17 @@ def tile_selfattention_kernel(tc, k_cache, q, v, offs, out):
         inverse_sum = [held.tile([P, 1], F32, name=f"inverse_sum{b}") for b in range(BLOCKS)]
         for b in range(BLOCKS):
             weight_sum = held.tile([P, 1], F32, name=f"weight_sum{b}")
+            last = b == BLOCKS - 1
             nc.scalar.activation(
                 weights[b][:],
                 raw[b][:],
                 EXP,
                 bias=minus_max[b][:],
                 scale=query_scale[:, b : b + 1],
-                accum_out=weight_sum[:],
+                accum_out=weight_sum[:] if last else None,
             )
+            if not last:
+                nc.vector.reduce_sum(weight_sum[:], weights[b][:], axis=X)
             nc.vector.reciprocal(inverse_sum[b][:], weight_sum[:])
         weights_by_entry = [held.tile([N, P], BF16, name=f"weights_by_entry{b}") for b in range(BLOCKS)]
         for b in range(BLOCKS):

import concourse.mybir as mybir
from concourse.masks import make_identity

BF16, F32, U16 = mybir.dt.bfloat16, mybir.dt.float32, mybir.dt.uint16
ADD, MULT, POW = (
    mybir.AluOpType.add,
    mybir.AluOpType.mult,
    mybir.AluOpType.pow,
)
EXP = mybir.ActivationFunctionType.Exp
X = mybir.AxisListType.X

P = 128
S, HD, M, N = 512, 128, 256, 128
BLOCKS = M // P
CHUNKS = S // P
EPS = 1e-6
FLOPS = 2 * M * N * HD * 2


def tile_selfattention_kernel(tc, k_cache, q, v, offs, out):
    nc = tc.nc
    with (
        tc.tile_pool(name="held", bufs=1) as held,
        tc.psum_pool(name="turn", bufs=2) as turn,
        tc.psum_pool(name="acc", bufs=1) as acc,
    ):
        queries = held.tile([HD, M], BF16, name="queries")
        nc.sync.dma_start(queries[:], q)
        load_queue = (nc.scalar, nc.sync)
        key_rows = [held.tile([P, HD], BF16, name=f"key_rows{c}") for c in range(CHUNKS)]
        for c in range(CHUNKS):
            load_queue[c % 2].dma_start(key_rows[c][:], k_cache[c * P : (c + 1) * P, :])
        offsets = held.tile([P, N // 16], U16, name="offsets")
        nc.sync.dma_start(offsets[:], offs)
        values = held.tile([N, HD], BF16, name="values")
        nc.sync.dma_start(values[:], v)

        identity = held.tile([P, P], BF16, name="identity")
        make_identity(nc, identity[:])
        minus_half = held.tile([P, BLOCKS], F32, name="minus_half")
        nc.vector.memset(minus_half[:], -0.5)

        table_primer = held.tile([P, BLOCKS], F32, name="table_primer")
        nc.scalar.activation(table_primer[:], minus_half[:], EXP)

        shifted_sums = held.tile([P, BLOCKS], F32, name="shifted_sums")
        for b in range(BLOCKS):
            q_b = queries[:, b * P : (b + 1) * P]
            products = turn.tile([P, P], F32, name=f"products{b}", tag="turn")
            nc.tensor.matmul(products[:], q_b, q_b, start=True, stop=True)
            diagonal = held.tile([P, P], F32, name=f"diagonal{b}")
            nc.vector.scalar_tensor_tensor(
                diagonal[:], products[:], HD * EPS, identity[:], ADD, MULT, accum_out=shifted_sums[:, b : b + 1]
            )
        query_scale = held.tile([P, BLOCKS], F32, name="query_scale")
        nc.gpsimd.tensor_tensor(query_scale[:], shifted_sums[:], minus_half[:], POW)

        key_window = held.tile([HD, S], BF16, name="key_window")
        for h in range(CHUNKS // 2):
            flipped_keys = acc.tile([HD, 2 * P], BF16, name=f"flipped_keys{h}")
            for c in range(2):
                nc.tensor.transpose(flipped_keys[:, c * P : (c + 1) * P], key_rows[2 * h + c][:], identity[:])
            nc.vector.tensor_copy(key_window[:, h * 2 * P : (h + 1) * 2 * P], flipped_keys[:])

        raw = [acc.tile([P, N], F32, name=f"raw{b}") for b in range(BLOCKS)]
        for b in range(BLOCKS):
            nc.tensor.matmul(
                raw[b][:], queries[:, b * P : (b + 1) * P], key_window[:].indirect(offsets[:]), start=True, stop=True
            )
        minus_max = [held.tile([P, 1], F32, name=f"minus_max{b}") for b in range(BLOCKS)]
        for b in range(BLOCKS):
            raw_max = held.tile([P, 1], F32, name=f"raw_max{b}")
            nc.vector.reduce_max(raw_max[:], raw[b][:], axis=X)
            nc.vector.tensor_scalar(minus_max[b][:], raw_max[:], query_scale[:, b : b + 1], -1.0, MULT, MULT)
        weights = [held.tile([P, N], BF16, name=f"weights{b}") for b in range(BLOCKS)]
        inverse_sum = [held.tile([P, 1], F32, name=f"inverse_sum{b}") for b in range(BLOCKS)]
        for b in range(BLOCKS):
            weight_sum = held.tile([P, 1], F32, name=f"weight_sum{b}")
            last = b == BLOCKS - 1
            nc.scalar.activation(
                weights[b][:],
                raw[b][:],
                EXP,
                bias=minus_max[b][:],
                scale=query_scale[:, b : b + 1],
                accum_out=weight_sum[:] if last else None,
            )
            if not last:
                nc.vector.reduce_sum(weight_sum[:], weights[b][:], axis=X)
            nc.vector.reciprocal(inverse_sum[b][:], weight_sum[:])
        weights_by_entry = [held.tile([N, P], BF16, name=f"weights_by_entry{b}") for b in range(BLOCKS)]
        for b in range(BLOCKS):
            flipped_weights = turn.tile([N, P], BF16, name=f"flipped_weights{b}", tag="turn")
            nc.tensor.matmul(flipped_weights[:], weights[b][:], identity[:], start=True, stop=True)
            nc.vector.tensor_copy(weights_by_entry[b][:], flipped_weights[:])
        mixed = [acc.tile([P, HD], F32, name=f"mixed{b}") for b in range(BLOCKS)]
        for b in range(BLOCKS):
            nc.tensor.matmul(mixed[b][:], weights_by_entry[b][:], values[:], start=True, stop=True)
        result = held.tile([P, BLOCKS, HD], F32, name="result")
        for b in range(BLOCKS):
            nc.vector.tensor_scalar_mul(result[:, b, :], mixed[b][:], inverse_sum[b][:])
        nc.scalar.dma_start(out.rearrange("(b p) e -> p b e", p=P), result[:])
